import numpy as np
import ml_dtypes

BF16 = ml_dtypes.bfloat16


def bf(x):
    return np.asarray(x, np.float32).astype(BF16)


def f32(x):
    return np.asarray(x, np.float32)


def f64(x):
    return np.asarray(x).astype(np.float64)


def striped(idx):
    return np.tile(idx.reshape(-1, 16).T, (8, 1))


V, D, M, H, T, B, N = 4096, 128, 512, 2048, 16, 128, 2048


def setup_inputs():
    return {
        "table": bf(2.0 * np.random.standard_normal((D, V))),
        "w1": bf(2.0 * np.random.standard_normal((D, M)) / np.sqrt(D)),
        "b1": f32(0.1 * np.random.standard_normal((M, 1))),
        "scores": f32(np.random.uniform(0.0, 1.0, (1, N))),
        "w2": bf(np.random.standard_normal((M, H)) / np.sqrt(M)),
        "b2": f32(0.1 * np.random.standard_normal((H, 1))),
        "w3": bf(np.random.standard_normal((H, H)) / np.sqrt(H)),
        "b3": f32(0.1 * np.random.standard_normal((H, 1))),
        "w4": bf(np.random.standard_normal((H, H)) / np.sqrt(H)),
        "b4": f32(0.1 * np.random.standard_normal((H, 1))),
        "w5": bf(np.random.standard_normal((H, H)) / np.sqrt(H)),
        "b5": f32(0.1 * np.random.standard_normal((H, 1))),
        "offs": striped(np.random.permutation(np.tile(np.arange(V), 2))[:N]),
    }


def reference(table, w1, b1, scores, w2, b2, w3, b3, w4, b4, w5, b5, offs):
    idx = offs[:16].T.reshape(-1)
    p = f64(w1).T @ f64(table)[:, idx]
    h = (p * f64(scores)).reshape(M, B, T).mean(axis=2) + f64(b1)
    h = f64(w2).T @ h + f64(b2)
    h = f64(w3).T @ h + f64(b3)
    h = f64(w4).T @ h + f64(b4)
    h = f64(w5).T @ h + f64(b5)
    return h

@@ -1,0 +1,125 @@
+import concourse.mybir as mybir
+from concourse.masks import make_identity
+
+BF16, F32, U16 = mybir.dt.bfloat16, mybir.dt.float32, mybir.dt.uint16
+MULT, ADD = mybir.AluOpType.mult, mybir.AluOpType.add
+IDENTITY = mybir.ActivationFunctionType.Identity
+
+P = 128
+V, M, H = 4096, 512, 2048
+N, T, B = 2048, 16, 128
+PIECE = 512
+BANK = 512
+PER_BANK = BANK // B
+ROWS_PER_LOAD = 2
+LOADS_AHEAD = 20
+
+FLOPS = 2 * (P * M * N + M * H * B + 3 * H * H * B)
+
+
+def tile_dnn_b_kernel(tc, table, w1, b1, scores, w2, b2, w3, b3, w4, b4, w5, b5, offs, out):
+    nc = tc.nc
+    with (
+        tc.tile_pool(name="held", bufs=1) as held,
+        tc.tile_pool(name="weights", bufs=LOADS_AHEAD) as weights,
+        tc.tile_pool(name="work", bufs=2) as work,
+        tc.tile_pool(name="staging", bufs=4) as staging,
+        tc.psum_pool(name="psum", bufs=8) as psum,
+    ):
+        offsets = held.tile([P, N // 16], U16, name="offsets")
+        nc.sync.dma_start(offsets[:], offs)
+        w1_sb = held.tile([P, M], BF16, name="w1_sb")
+        nc.sync.dma_start(w1_sb[:], w1)
+        table_sb = held.tile([P, V], BF16, name="table_sb")
+        nc.sync.dma_start(table_sb[:], table)
+        scores_bc = held.tile([P, N], F32, name="scores_bc")
+        scores_row = scores.rearrange("o n -> (o n)")
+        for piece in range(N // PIECE):
+            cols = slice(piece * PIECE, (piece + 1) * PIECE)
+            nc.sync.dma_start(scores_bc[:, cols], scores_row[cols].partition_broadcast(P))
+
+        wanted = [(w, g) for w in (w2, w3, w4, w5) for g in range(w.shape[0] // (ROWS_PER_LOAD * P))]
+        loaded = []
+
+        def load_next():
+            if len(loaded) < len(wanted):
+                w, g = wanted[len(loaded)]
+                w_rows = weights.tile([P, ROWS_PER_LOAD, H], BF16, name="w_rows")
+                nc.sync.dma_start(w_rows[:], w.rearrange("(g k p) u -> g p k u", k=ROWS_PER_LOAD, p=P)[g])
+                loaded.append(w_rows)
+
+        for i in range(LOADS_AHEAD):
+            load_next()
+
+        bias_rows = held.tile([P, P], F32, name="bias_rows")
+        nc.vector.memset(bias_rows[:], 0.0)
+        first_row = {}
+        row = 0
+        for name, b in (("b2", b2), ("b3", b3), ("b4", b4), ("b5", b5), ("b1", b1)):
+            n_rows = b.shape[0] // P
+            nc.scalar.dma_start(bias_rows[row : row + n_rows, :], b.rearrange("(c p) o -> c (p o)", p=P))
+            first_row[name] = row
+            row += n_rows
+        ident = held.tile([P, P], F32, name="ident")
+        make_identity(nc, ident[:])
+        flipped = psum.tile([P, BANK], F32, name="flipped", tag="bank")
+        nc.tensor.transpose(flipped[:, :P], bias_rows[:], ident[:])
+        bias_cols = held.tile([P, P], F32, name="bias_cols")
+        nc.vector.tensor_copy(bias_cols[:], flipped[:, :P])
+
+        h1 = held.tile([P, M // P, B], BF16, name="h1")
+        for mb in range(M // P):
+            weighted = work.tile([P, N], F32, name="weighted")
+            for piece in range(N // PIECE):
+                cols = slice(piece * PIECE, (piece + 1) * PIECE)
+                projected = psum.tile([P, BANK], F32, name="projected", tag="bank")
+                nc.tensor.matmul(
+                    projected[:],
+                    w1_sb[:, mb * P : (mb + 1) * P],
+                    table_sb[:].indirect(offsets[:, piece * (PIECE // 16) : (piece + 1) * (PIECE // 16)]),
+                    start=True,
+                    stop=True,
+                )
+                nc.vector.tensor_tensor(weighted[:, cols], projected[:], scores_bc[:, cols], MULT)
+            sums = work.tile([P, B], F32, name="sums")
+            nc.vector.tensor_reduce(
+                sums[:], weighted[:].rearrange("p (n t) -> p n t", t=T), axis=mybir.AxisListType.X, op=ADD
+            )
+            b1_col = bias_cols[:, first_row["b1"] + mb : first_row["b1"] + mb + 1]
+            nc.scalar.activation(h1[:, mb, :], sums[:], IDENTITY, bias=b1_col, scale=1.0 / T)
+
+        def linear(h_in, first_load, bias_name, h_out):
+            n_in = h_in.shape[1]
+            banks = [psum.tile([P, BANK], F32, name=f"acc{b}", tag="bank") for b in range(H // BANK)]
+            for kb in range(n_in):
+                w_rows = loaded[first_load + kb // ROWS_PER_LOAD]
+                for c in range(H // P):
+                    nc.tensor.matmul(
+                        banks[c // PER_BANK][:, (c % PER_BANK) * B : (c % PER_BANK + 1) * B],
+                        w_rows[:, kb % ROWS_PER_LOAD, c * P : (c + 1) * P],
+                        h_in[:, kb, :],
+                        start=(kb == 0 and c % PER_BANK == 0),
+                        stop=(kb == n_in - 1 and c % PER_BANK == PER_BANK - 1),
+                    )
+                if kb % ROWS_PER_LOAD == ROWS_PER_LOAD - 1:
+                    load_next()
+            for b in range(H // BANK):
+                blocks = slice(b * PER_BANK, (b + 1) * PER_BANK)
+                acc = banks[b][:].rearrange("p (c n) -> p c n", c=PER_BANK)
+                c0 = first_row[bias_name] + b * PER_BANK
+                bias = bias_cols[:, c0 : c0 + PER_BANK].unsqueeze(2).to_broadcast([P, PER_BANK, B])
+                if h_out is None:
+                    staged = staging.tile([P, PER_BANK, B], F32, name="staged")
+                    nc.vector.tensor_tensor(staged[:], acc, bias, ADD)
+                    nc.sync.dma_start(out.rearrange("(c p) n -> p c n", p=P)[:, blocks, :], staged[:])
+                else:
+                    nc.vector.tensor_tensor(h_out[:, blocks, :], acc, bias, ADD)
+            return first_load + n_in // ROWS_PER_LOAD
+
+        h2 = held.tile([P, H // P, B], BF16, name="h2")
+        h3 = held.tile([P, H // P, B], BF16, name="h3")
+        h4 = held.tile([P, H // P, B], BF16, name="h4")
+        load = linear(h1, 0, "b2", h2)
+        load = linear(h2, load, "b3", h3)
+        load = linear(h3, load, "b4", h4)
+        linear(h4, load, "b5", None)

@@ -13,6 +13,7 @@ BANK = 512
 PER_BANK = BANK // B
 ROWS_PER_LOAD = 2
 LOADS_AHEAD = 20
+SUM_LAG = 3
 
 FLOPS = 2 * (P * M * N + M * H * B + 3 * H * H * B)
 
@@ -22,7 +23,7 @@ def tile_dnn_b_kernel(tc, table, w1, b1, scores, w2, b2, w3, b3, w4, b4, w5, b5,
     with (
         tc.tile_pool(name="held", bufs=1) as held,
         tc.tile_pool(name="weights", bufs=LOADS_AHEAD) as weights,
-        tc.tile_pool(name="work", bufs=2) as work,
+        tc.tile_pool(name="work", bufs=2 * SUM_LAG) as work,
         tc.tile_pool(name="staging", bufs=4) as staging,
         tc.psum_pool(name="psum", bufs=8) as psum,
     ):
@@ -68,9 +69,13 @@ def tile_dnn_b_kernel(tc, table, w1, b1, scores, w2, b2, w3, b3, w4, b4, w5, b5,
         nc.vector.tensor_copy(bias_cols[:], flipped[:, :P])
 
         h1 = held.tile([P, M // P, B], BF16, name="h1")
-        for mb in range(M // P):
-            weighted = work.tile([P, N], F32, name="weighted")
-            for piece in range(N // PIECE):
+        n_pieces = N // PIECE
+        n_units = (M // P) * n_pieces
+        weighted_of = {}
+        sums_of = {}
+        for i in range(n_units + SUM_LAG):
+            if i < n_units:
+                mb, piece = divmod(i, n_pieces)
                 cols = slice(piece * PIECE, (piece + 1) * PIECE)
                 projected = psum.tile([P, BANK], F32, name="projected", tag="bank")
                 nc.tensor.matmul(
@@ -80,13 +85,27 @@ def tile_dnn_b_kernel(tc, table, w1, b1, scores, w2, b2, w3, b3, w4, b4, w5, b5,
                     start=True,
                     stop=True,
                 )
-                nc.vector.tensor_tensor(weighted[:, cols], projected[:], scores_bc[:, cols], MULT)
-            sums = work.tile([P, B], F32, name="sums")
-            nc.vector.tensor_reduce(
-                sums[:], weighted[:].rearrange("p (n t) -> p n t", t=T), axis=mybir.AxisListType.X, op=ADD
-            )
-            b1_col = bias_cols[:, first_row["b1"] + mb : first_row["b1"] + mb + 1]
-            nc.scalar.activation(h1[:, mb, :], sums[:], IDENTITY, bias=b1_col, scale=1.0 / T)
+                weighted = work.tile([P, PIECE], F32, name="weighted")
+                if i % 3 == 0:
+                    nc.vector.tensor_tensor(weighted[:], projected[:], scores_bc[:, cols], MULT)
+                else:
+                    copied = work.tile([P, PIECE], F32, name="copied")
+                    nc.scalar.copy(copied[:], projected[:])
+                    nc.gpsimd.tensor_tensor(weighted[:], copied[:], scores_bc[:, cols], MULT)
+                weighted_of[i] = weighted
+            if i >= SUM_LAG:
+                mb, piece = divmod(i - SUM_LAG, n_pieces)
+                if piece == 0:
+                    sums_of[mb] = work.tile([P, B], F32, name="sums")
+                nc.vector.tensor_reduce(
+                    sums_of[mb][:, piece * (PIECE // T) : (piece + 1) * (PIECE // T)],
+                    weighted_of[i - SUM_LAG][:].rearrange("p (n t) -> p n t", t=T),
+                    axis=mybir.AxisListType.X,
+                    op=ADD,
+                )
+                if piece == n_pieces - 1:
+                    b1_col = bias_cols[:, first_row["b1"] + mb : first_row["b1"] + mb + 1]
+                    nc.scalar.activation(h1[:, mb, :], sums_of[mb][:], IDENTITY, bias=b1_col, scale=1.0 / T)
 
         def linear(h_in, first_load, bias_name, h_out):
             n_in = h_in.shape[1]

@@ -86,7 +86,7 @@ def tile_dnn_b_kernel(tc, table, w1, b1, scores, w2, b2, w3, b3, w4, b4, w5, b5,
                     stop=True,
                 )
                 weighted = work.tile([P, PIECE], F32, name="weighted")
-                if i % 3 == 0:
+                if i % 2 == 0:
                     nc.vector.tensor_tensor(weighted[:], projected[:], scores_bc[:, cols], MULT)
                 else:
                     copied = work.tile([P, PIECE], F32, name="copied")

@@ -63,10 +63,7 @@ def tile_dnn_b_kernel(tc, table, w1, b1, scores, w2, b2, w3, b3, w4, b4, w5, b5,
             row += n_rows
         ident = held.tile([P, P], F32, name="ident")
         make_identity(nc, ident[:])
-        flipped = psum.tile([P, BANK], F32, name="flipped", tag="bank")
-        nc.tensor.transpose(flipped[:, :P], bias_rows[:], ident[:])
         bias_cols = held.tile([P, P], F32, name="bias_cols")
-        nc.vector.tensor_copy(bias_cols[:], flipped[:, :P])
 
         h1 = held.tile([P, M // P, B], BF16, name="h1")
         n_pieces = N // PIECE
@@ -93,6 +90,10 @@ def tile_dnn_b_kernel(tc, table, w1, b1, scores, w2, b2, w3, b3, w4, b4, w5, b5,
                     nc.scalar.copy(copied[:], projected[:])
                     nc.gpsimd.tensor_tensor(weighted[:], copied[:], scores_bc[:, cols], MULT)
                 weighted_of[i] = weighted
+            if i == SUM_LAG - 1:
+                flipped = psum.tile([P, BANK], F32, name="flipped", tag="bank")
+                nc.tensor.transpose(flipped[:, :P], bias_rows[:], ident[:])
+                nc.vector.tensor_copy(bias_cols[:], flipped[:, :P])
             if i >= SUM_LAG:
                 mb, piece = divmod(i - SUM_LAG, n_pieces)
                 if piece == 0:
@@ -107,20 +108,23 @@ def tile_dnn_b_kernel(tc, table, w1, b1, scores, w2, b2, w3, b3, w4, b4, w5, b5,
                     b1_col = bias_cols[:, first_row["b1"] + mb : first_row["b1"] + mb + 1]
                     nc.scalar.activation(h1[:, mb, :], sums_of[mb][:], IDENTITY, bias=b1_col, scale=1.0 / T)
 
-        def linear(h_in, first_load, bias_name, h_out):
+        def linear(h_in, first_load, bias_name, h_out, together):
             n_in = h_in.shape[1]
             banks = [psum.tile([P, BANK], F32, name=f"acc{b}", tag="bank") for b in range(H // BANK)]
-            for kb in range(n_in):
-                w_rows = loaded[first_load + kb // ROWS_PER_LOAD]
-                for c in range(H // P):
-                    nc.tensor.matmul(
-                        banks[c // PER_BANK][:, (c % PER_BANK) * B : (c % PER_BANK + 1) * B],
-                        w_rows[:, kb % ROWS_PER_LOAD, c * P : (c + 1) * P],
-                        h_in[:, kb, :],
-                        start=(kb == 0 and c % PER_BANK == 0),
-                        stop=(kb == n_in - 1 and c % PER_BANK == PER_BANK - 1),
-                    )
-                if kb % ROWS_PER_LOAD == ROWS_PER_LOAD - 1:
+            for first_kb in range(0, n_in, together):
+                for b in range(H // BANK):
+                    for kb in range(first_kb, first_kb + together):
+                        w_rows = loaded[first_load + kb // ROWS_PER_LOAD]
+                        for j in range(PER_BANK):
+                            c = b * PER_BANK + j
+                            nc.tensor.matmul(
+                                banks[b][:, j * B : (j + 1) * B],
+                                w_rows[:, kb % ROWS_PER_LOAD, c * P : (c + 1) * P],
+                                h_in[:, kb, :],
+                                start=(kb == 0 and j == 0),
+                                stop=(kb == n_in - 1 and j == PER_BANK - 1),
+                            )
+                if (first_kb + together) % ROWS_PER_LOAD == 0:
                     load_next()
             for b in range(H // BANK):
                 blocks = slice(b * PER_BANK, (b + 1) * PER_BANK)
@@ -138,7 +142,7 @@ def tile_dnn_b_kernel(tc, table, w1, b1, scores, w2, b2, w3, b3, w4, b4, w5, b5,
         h2 = held.tile([P, H // P, B], BF16, name="h2")
         h3 = held.tile([P, H // P, B], BF16, name="h3")
         h4 = held.tile([P, H // P, B], BF16, name="h4")
-        load = linear(h1, 0, "b2", h2)
-        load = linear(h2, load, "b3", h3)
-        load = linear(h3, load, "b4", h4)
-        linear(h4, load, "b5", None)
+        load = linear(h1, 0, "b2", h2, 1)
+        load = linear(h2, load, "b3", h3, ROWS_PER_LOAD)
+        load = linear(h3, load, "b4", h4, ROWS_PER_LOAD)
+        linear(h4, load, "b5", None, ROWS_PER_LOAD)

@@ -24,6 +24,7 @@ def tile_dnn_b_kernel(tc, table, w1, b1, scores, w2, b2, w3, b3, w4, b4, w5, b5,
         tc.tile_pool(name="held", bufs=1) as held,
         tc.tile_pool(name="weights", bufs=LOADS_AHEAD) as weights,
         tc.tile_pool(name="work", bufs=2 * SUM_LAG) as work,
+        tc.tile_pool(name="scrap", bufs=2) as scrap,
         tc.tile_pool(name="staging", bufs=4) as staging,
         tc.psum_pool(name="psum", bufs=8) as psum,
     ):
@@ -98,12 +99,24 @@ def tile_dnn_b_kernel(tc, table, w1, b1, scores, w2, b2, w3, b3, w4, b4, w5, b5,
                 mb, piece = divmod(i - SUM_LAG, n_pieces)
                 if piece == 0:
                     sums_of[mb] = work.tile([P, B], F32, name="sums")
-                nc.vector.tensor_reduce(
-                    sums_of[mb][:, piece * (PIECE // T) : (piece + 1) * (PIECE // T)],
-                    weighted_of[i - SUM_LAG][:].rearrange("p (n t) -> p n t", t=T),
-                    axis=mybir.AxisListType.X,
-                    op=ADD,
-                )
+                first = piece * (PIECE // T)
+                if piece == 0:
+                    passed = scrap.tile([P, PIECE], F32, name="passed")
+                    for n in range(PIECE // T):
+                        words = slice(n * T, (n + 1) * T)
+                        nc.scalar.activation(
+                            passed[:, words],
+                            weighted_of[i - SUM_LAG][:, words],
+                            IDENTITY,
+                            accum_out=sums_of[mb][:, first + n : first + n + 1],
+                        )
+                else:
+                    nc.vector.tensor_reduce(
+                        sums_of[mb][:, first : first + PIECE // T],
+                        weighted_of[i - SUM_LAG][:].rearrange("p (n t) -> p n t", t=T),
+                        axis=mybir.AxisListType.X,
+                        op=ADD,
+                    )
                 if piece == n_pieces - 1:
                     b1_col = bias_cols[:, first_row["b1"] + mb : first_row["b1"] + mb + 1]
                     nc.scalar.activation(h1[:, mb, :], sums_of[mb][:], IDENTITY, bias=b1_col, scale=1.0 / T)

@@ -13,6 +13,7 @@ BANK = 512
 PER_BANK = BANK // B
 ROWS_PER_LOAD = 2
 LOADS_AHEAD = 20
+SCALAR_SENTENCES = 16
 SUM_LAG = 3
 
 FLOPS = 2 * (P * M * N + M * H * B + 3 * H * H * B)
@@ -100,9 +101,10 @@ def tile_dnn_b_kernel(tc, table, w1, b1, scores, w2, b2, w3, b3, w4, b4, w5, b5,
                 if piece == 0:
                     sums_of[mb] = work.tile([P, B], F32, name="sums")
                 first = piece * (PIECE // T)
-                if piece == 0:
-                    passed = scrap.tile([P, PIECE], F32, name="passed")
-                    for n in range(PIECE // T):
+                by_scalar = SCALAR_SENTENCES if piece == 0 else 0
+                if by_scalar:
+                    passed = scrap.tile([P, by_scalar * T], F32, name="passed")
+                    for n in range(by_scalar):
                         words = slice(n * T, (n + 1) * T)
                         nc.scalar.activation(
                             passed[:, words],
@@ -110,13 +112,12 @@ def tile_dnn_b_kernel(tc, table, w1, b1, scores, w2, b2, w3, b3, w4, b4, w5, b5,
                             IDENTITY,
                             accum_out=sums_of[mb][:, first + n : first + n + 1],
                         )
-                else:
-                    nc.vector.tensor_reduce(
-                        sums_of[mb][:, first : first + PIECE // T],
-                        weighted_of[i - SUM_LAG][:].rearrange("p (n t) -> p n t", t=T),
-                        axis=mybir.AxisListType.X,
-                        op=ADD,
-                    )
+                nc.vector.tensor_reduce(
+                    sums_of[mb][:, first + by_scalar : first + PIECE // T],
+                    weighted_of[i - SUM_LAG][:, by_scalar * T :].rearrange("p (n t) -> p n t", t=T),
+                    axis=mybir.AxisListType.X,
+                    op=ADD,
+                )
                 if piece == n_pieces - 1:
                     b1_col = bias_cols[:, first_row["b1"] + mb : first_row["b1"] + mb + 1]
                     nc.scalar.activation(h1[:, mb, :], sums_of[mb][:], IDENTITY, bias=b1_col, scale=1.0 / T)

@@ -11,10 +11,11 @@ N, T, B = 2048, 16, 128
 PIECE = 512
 BANK = 512
 PER_BANK = BANK // B
+PER_BANK_LAST = 2
 ROWS_PER_LOAD = 2
 LOADS_AHEAD = 20
-SCALAR_SENTENCES = 16
-SUM_LAG = 3
+SCALAR_SENTENCES = 3
+SUM_LAG = 4
 
 FLOPS = 2 * (P * M * N + M * H * B + 3 * H * H * B)
 
@@ -26,7 +27,7 @@ def tile_dnn_b_kernel(tc, table, w1, b1, scores, w2, b2, w3, b3, w4, b4, w5, b5,
         tc.tile_pool(name="weights", bufs=LOADS_AHEAD) as weights,
         tc.tile_pool(name="work", bufs=2 * SUM_LAG) as work,
         tc.tile_pool(name="scrap", bufs=2) as scrap,
-        tc.tile_pool(name="staging", bufs=4) as staging,
+        tc.tile_pool(name="staging", bufs=8) as staging,
         tc.psum_pool(name="psum", bufs=8) as psum,
     ):
         offsets = held.tile([P, N // 16], U16, name="offsets")
@@ -101,20 +102,18 @@ def tile_dnn_b_kernel(tc, table, w1, b1, scores, w2, b2, w3, b3, w4, b4, w5, b5,
                 if piece == 0:
                     sums_of[mb] = work.tile([P, B], F32, name="sums")
                 first = piece * (PIECE // T)
-                by_scalar = SCALAR_SENTENCES if piece == 0 else 0
-                if by_scalar:
-                    passed = scrap.tile([P, by_scalar * T], F32, name="passed")
-                    for n in range(by_scalar):
-                        words = slice(n * T, (n + 1) * T)
-                        nc.scalar.activation(
-                            passed[:, words],
-                            weighted_of[i - SUM_LAG][:, words],
-                            IDENTITY,
-                            accum_out=sums_of[mb][:, first + n : first + n + 1],
-                        )
+                passed = scrap.tile([P, SCALAR_SENTENCES * T], F32, name="passed")
+                for n in range(SCALAR_SENTENCES):
+                    words = slice(n * T, (n + 1) * T)
+                    nc.scalar.activation(
+                        passed[:, words],
+                        weighted_of[i - SUM_LAG][:, words],
+                        IDENTITY,
+                        accum_out=sums_of[mb][:, first + n : first + n + 1],
+                    )
                 nc.vector.tensor_reduce(
-                    sums_of[mb][:, first + by_scalar : first + PIECE // T],
-                    weighted_of[i - SUM_LAG][:, by_scalar * T :].rearrange("p (n t) -> p n t", t=T),
+                    sums_of[mb][:, first + SCALAR_SENTENCES : first + PIECE // T],
+                    weighted_of[i - SUM_LAG][:, SCALAR_SENTENCES * T :].rearrange("p (n t) -> p n t", t=T),
                     axis=mybir.AxisListType.X,
                     op=ADD,
                 )
@@ -122,32 +121,42 @@ def tile_dnn_b_kernel(tc, table, w1, b1, scores, w2, b2, w3, b3, w4, b4, w5, b5,
                     b1_col = bias_cols[:, first_row["b1"] + mb : first_row["b1"] + mb + 1]
                     nc.scalar.activation(h1[:, mb, :], sums_of[mb][:], IDENTITY, bias=b1_col, scale=1.0 / T)
 
-        def linear(h_in, first_load, bias_name, h_out, together):
+        def linear(h_in, first_load, bias_name, h_out, together, per_bank):
             n_in = h_in.shape[1]
-            banks = [psum.tile([P, BANK], F32, name=f"acc{b}", tag="bank") for b in range(H // BANK)]
+            n_banks = H // P // per_bank
+            banks = [psum.tile([P, per_bank * B], F32, name=f"acc{b}", tag="bank") for b in range(n_banks)]
             for first_kb in range(0, n_in, together):
-                for b in range(H // BANK):
+                for b in range(n_banks):
                     for kb in range(first_kb, first_kb + together):
                         w_rows = loaded[first_load + kb // ROWS_PER_LOAD]
-                        for j in range(PER_BANK):
-                            c = b * PER_BANK + j
+                        for j in range(per_bank):
+                            c = b * per_bank + j
                             nc.tensor.matmul(
                                 banks[b][:, j * B : (j + 1) * B],
                                 w_rows[:, kb % ROWS_PER_LOAD, c * P : (c + 1) * P],
                                 h_in[:, kb, :],
                                 start=(kb == 0 and j == 0),
-                                stop=(kb == n_in - 1 and j == PER_BANK - 1),
+                                stop=(kb == n_in - 1 and j == per_bank - 1),
                             )
                 if (first_kb + together) % ROWS_PER_LOAD == 0:
                     load_next()
-            for b in range(H // BANK):
-                blocks = slice(b * PER_BANK, (b + 1) * PER_BANK)
-                acc = banks[b][:].rearrange("p (c n) -> p c n", c=PER_BANK)
-                c0 = first_row[bias_name] + b * PER_BANK
-                bias = bias_cols[:, c0 : c0 + PER_BANK].unsqueeze(2).to_broadcast([P, PER_BANK, B])
+            for b in range(n_banks):
+                blocks = slice(b * per_bank, (b + 1) * per_bank)
+                acc = banks[b][:].rearrange("p (c n) -> p c n", c=per_bank)
+                c0 = first_row[bias_name] + b * per_bank
+                bias = bias_cols[:, c0 : c0 + per_bank].unsqueeze(2).to_broadcast([P, per_bank, B])
                 if h_out is None:
-                    staged = staging.tile([P, PER_BANK, B], F32, name="staged")
-                    nc.vector.tensor_tensor(staged[:], acc, bias, ADD)
+                    staged = staging.tile([P, per_bank, B], F32, name="staged")
+                    if b % 2 == 0:
+                        for j in range(per_bank):
+                            nc.scalar.activation(
+                                staged[:, j, :],
+                                banks[b][:, j * B : (j + 1) * B],
+                                IDENTITY,
+                                bias=bias_cols[:, c0 + j : c0 + j + 1],
+                            )
+                    else:
+                        nc.vector.tensor_tensor(staged[:], acc, bias, ADD)
                     nc.sync.dma_start(out.rearrange("(c p) n -> p c n", p=P)[:, blocks, :], staged[:])
                 else:
                     nc.vector.tensor_tensor(h_out[:, blocks, :], acc, bias, ADD)
@@ -156,7 +165,7 @@ def tile_dnn_b_kernel(tc, table, w1, b1, scores, w2, b2, w3, b3, w4, b4, w5, b5,
         h2 = held.tile([P, H // P, B], BF16, name="h2")
         h3 = held.tile([P, H // P, B], BF16, name="h3")
         h4 = held.tile([P, H // P, B], BF16, name="h4")
-        load = linear(h1, 0, "b2", h2, 1)
-        load = linear(h2, load, "b3", h3, ROWS_PER_LOAD)
-        load = linear(h3, load, "b4", h4, ROWS_PER_LOAD)
-        linear(h4, load, "b5", None, ROWS_PER_LOAD)
+        load = linear(h1, 0, "b2", h2, 1, PER_BANK)
+        load = linear(h2, load, "b3", h3, ROWS_PER_LOAD, PER_BANK)
+        load = linear(h3, load, "b4", h4, ROWS_PER_LOAD, PER_BANK)
+        linear(h4, load, "b5", None, ROWS_PER_LOAD, PER_BANK_LAST)

@@ -15,7 +15,8 @@ PER_BANK_LAST = 2
 ROWS_PER_LOAD = 2
 LOADS_AHEAD = 20
 SCALAR_SENTENCES = 3
-SUM_LAG = 4
+VECTOR_LAG = 1
+GPSIMD_LAG = 4
 
 FLOPS = 2 * (P * M * N + M * H * B + 3 * H * H * B)
 
@@ -25,7 +26,8 @@ def tile_dnn_b_kernel(tc, table, w1, b1, scores, w2, b2, w3, b3, w4, b4, w5, b5,
     with (
         tc.tile_pool(name="held", bufs=1) as held,
         tc.tile_pool(name="weights", bufs=LOADS_AHEAD) as weights,
-        tc.tile_pool(name="work", bufs=2 * SUM_LAG) as work,
+        tc.tile_pool(name="work", bufs=2 * GPSIMD_LAG) as work,
+        tc.tile_pool(name="copies", bufs=2) as copies,
         tc.tile_pool(name="scrap", bufs=2) as scrap,
         tc.tile_pool(name="staging", bufs=8) as staging,
         tc.psum_pool(name="psum", bufs=8) as psum,
@@ -73,7 +75,7 @@ def tile_dnn_b_kernel(tc, table, w1, b1, scores, w2, b2, w3, b3, w4, b4, w5, b5,
         n_units = (M // P) * n_pieces
         weighted_of = {}
         sums_of = {}
-        for i in range(n_units + SUM_LAG):
+        for i in range(n_units + GPSIMD_LAG):
             if i < n_units:
                 mb, piece = divmod(i, n_pieces)
                 cols = slice(piece * PIECE, (piece + 1) * PIECE)
@@ -89,16 +91,17 @@ def tile_dnn_b_kernel(tc, table, w1, b1, scores, w2, b2, w3, b3, w4, b4, w5, b5,
                 if i % 2 == 0:
                     nc.vector.tensor_tensor(weighted[:], projected[:], scores_bc[:, cols], MULT)
                 else:
-                    copied = work.tile([P, PIECE], F32, name="copied")
+                    copied = copies.tile([P, PIECE], F32, name="copied")
                     nc.scalar.copy(copied[:], projected[:])
                     nc.gpsimd.tensor_tensor(weighted[:], copied[:], scores_bc[:, cols], MULT)
                 weighted_of[i] = weighted
-            if i == SUM_LAG - 1:
+            if i == GPSIMD_LAG - 1:
                 flipped = psum.tile([P, BANK], F32, name="flipped", tag="bank")
                 nc.tensor.transpose(flipped[:, :P], bias_rows[:], ident[:])
                 nc.vector.tensor_copy(bias_cols[:], flipped[:, :P])
-            if i >= SUM_LAG:
-                mb, piece = divmod(i - SUM_LAG, n_pieces)
+            due = [k for k in range(n_units) if k + (VECTOR_LAG if k % 2 == 0 else GPSIMD_LAG) == i]
+            for k in due:
+                mb, piece = divmod(k, n_pieces)
                 if piece == 0:
                     sums_of[mb] = work.tile([P, B], F32, name="sums")
                 first = piece * (PIECE // T)
@@ -107,13 +110,13 @@ def tile_dnn_b_kernel(tc, table, w1, b1, scores, w2, b2, w3, b3, w4, b4, w5, b5,
                     words = slice(n * T, (n + 1) * T)
                     nc.scalar.activation(
                         passed[:, words],
-                        weighted_of[i - SUM_LAG][:, words],
+                        weighted_of[k][:, words],
                         IDENTITY,
                         accum_out=sums_of[mb][:, first + n : first + n + 1],
                     )
                 nc.vector.tensor_reduce(
                     sums_of[mb][:, first + SCALAR_SENTENCES : first + PIECE // T],
-                    weighted_of[i - SUM_LAG][:, SCALAR_SENTENCES * T :].rearrange("p (n t) -> p n t", t=T),
+                    weighted_of[k][:, SCALAR_SENTENCES * T :].rearrange("p (n t) -> p n t", t=T),
                     axis=mybir.AxisListType.X,
                     op=ADD,
                 )

import concourse.mybir as mybir
from concourse.masks import make_identity

BF16, F32, U16 = mybir.dt.bfloat16, mybir.dt.float32, mybir.dt.uint16
MULT, ADD = mybir.AluOpType.mult, mybir.AluOpType.add
IDENTITY = mybir.ActivationFunctionType.Identity

P = 128
V, M, H = 4096, 512, 2048
N, T, B = 2048, 16, 128
PIECE = 512
BANK = 512
PER_BANK = BANK // B
PER_BANK_LAST = 2
ROWS_PER_LOAD = 2
LOADS_AHEAD = 20
SCALAR_SENTENCES = 3
VECTOR_LAG = 1
GPSIMD_LAG = 4

FLOPS = 2 * (P * M * N + M * H * B + 3 * H * H * B)


def tile_dnn_b_kernel(tc, table, w1, b1, scores, w2, b2, w3, b3, w4, b4, w5, b5, offs, out):
    nc = tc.nc
    with (
        tc.tile_pool(name="held", bufs=1) as held,
        tc.tile_pool(name="weights", bufs=LOADS_AHEAD) as weights,
        tc.tile_pool(name="work", bufs=2 * GPSIMD_LAG) as work,
        tc.tile_pool(name="copies", bufs=2) as copies,
        tc.tile_pool(name="scrap", bufs=2) as scrap,
        tc.tile_pool(name="staging", bufs=8) as staging,
        tc.psum_pool(name="psum", bufs=8) as psum,
    ):
        offsets = held.tile([P, N // 16], U16, name="offsets")
        nc.sync.dma_start(offsets[:], offs)
        w1_sb = held.tile([P, M], BF16, name="w1_sb")
        nc.sync.dma_start(w1_sb[:], w1)
        table_sb = held.tile([P, V], BF16, name="table_sb")
        nc.sync.dma_start(table_sb[:], table)
        scores_bc = held.tile([P, N], F32, name="scores_bc")
        scores_row = scores.rearrange("o n -> (o n)")
        for piece in range(N // PIECE):
            cols = slice(piece * PIECE, (piece + 1) * PIECE)
            nc.sync.dma_start(scores_bc[:, cols], scores_row[cols].partition_broadcast(P))

        wanted = [(w, g) for w in (w2, w3, w4, w5) for g in range(w.shape[0] // (ROWS_PER_LOAD * P))]
        loaded = []

        def load_next():
            if len(loaded) < len(wanted):
                w, g = wanted[len(loaded)]
                w_rows = weights.tile([P, ROWS_PER_LOAD, H], BF16, name="w_rows")
                nc.sync.dma_start(w_rows[:], w.rearrange("(g k p) u -> g p k u", k=ROWS_PER_LOAD, p=P)[g])
                loaded.append(w_rows)

        for i in range(LOADS_AHEAD):
            load_next()

        bias_rows = held.tile([P, P], F32, name="bias_rows")
        nc.vector.memset(bias_rows[:], 0.0)
        first_row = {}
        row = 0
        for name, b in (("b2", b2), ("b3", b3), ("b4", b4), ("b5", b5), ("b1", b1)):
            n_rows = b.shape[0] // P
            nc.scalar.dma_start(bias_rows[row : row + n_rows, :], b.rearrange("(c p) o -> c (p o)", p=P))
            first_row[name] = row
            row += n_rows
        ident = held.tile([P, P], F32, name="ident")
        make_identity(nc, ident[:])
        bias_cols = held.tile([P, P], F32, name="bias_cols")

        h1 = held.tile([P, M // P, B], BF16, name="h1")
        n_pieces = N // PIECE
        n_units = (M // P) * n_pieces
        weighted_of = {}
        sums_of = {}
        for i in range(n_units + GPSIMD_LAG):
            if i < n_units:
                mb, piece = divmod(i, n_pieces)
                cols = slice(piece * PIECE, (piece + 1) * PIECE)
                projected = psum.tile([P, BANK], F32, name="projected", tag="bank")
                nc.tensor.matmul(
                    projected[:],
                    w1_sb[:, mb * P : (mb + 1) * P],
                    table_sb[:].indirect(offsets[:, piece * (PIECE // 16) : (piece + 1) * (PIECE // 16)]),
                    start=True,
                    stop=True,
                )
                weighted = work.tile([P, PIECE], F32, name="weighted")
                if i % 2 == 0:
                    nc.vector.tensor_tensor(weighted[:], projected[:], scores_bc[:, cols], MULT)
                else:
                    copied = copies.tile([P, PIECE], F32, name="copied")
                    nc.scalar.copy(copied[:], projected[:])
                    nc.gpsimd.tensor_tensor(weighted[:], copied[:], scores_bc[:, cols], MULT)
                weighted_of[i] = weighted
            if i == GPSIMD_LAG - 1:
                flipped = psum.tile([P, BANK], F32, name="flipped", tag="bank")
                nc.tensor.transpose(flipped[:, :P], bias_rows[:], ident[:])
                nc.vector.tensor_copy(bias_cols[:], flipped[:, :P])
            due = [k for k in range(n_units) if k + (VECTOR_LAG if k % 2 == 0 else GPSIMD_LAG) == i]
            for k in due:
                mb, piece = divmod(k, n_pieces)
                if piece == 0:
                    sums_of[mb] = work.tile([P, B], F32, name="sums")
                first = piece * (PIECE // T)
                passed = scrap.tile([P, SCALAR_SENTENCES * T], F32, name="passed")
                for n in range(SCALAR_SENTENCES):
                    words = slice(n * T, (n + 1) * T)
                    nc.scalar.activation(
                        passed[:, words],
                        weighted_of[k][:, words],
                        IDENTITY,
                        accum_out=sums_of[mb][:, first + n : first + n + 1],
                    )
                nc.vector.tensor_reduce(
                    sums_of[mb][:, first + SCALAR_SENTENCES : first + PIECE // T],
                    weighted_of[k][:, SCALAR_SENTENCES * T :].rearrange("p (n t) -> p n t", t=T),
                    axis=mybir.AxisListType.X,
                    op=ADD,
                )
                if piece == n_pieces - 1:
                    b1_col = bias_cols[:, first_row["b1"] + mb : first_row["b1"] + mb + 1]
                    nc.scalar.activation(h1[:, mb, :], sums_of[mb][:], IDENTITY, bias=b1_col, scale=1.0 / T)

        def linear(h_in, first_load, bias_name, h_out, together, per_bank):
            n_in = h_in.shape[1]
            n_banks = H // P // per_bank
            banks = [psum.tile([P, per_bank * B], F32, name=f"acc{b}", tag="bank") for b in range(n_banks)]
            for first_kb in range(0, n_in, together):
                for b in range(n_banks):
                    for kb in range(first_kb, first_kb + together):
                        w_rows = loaded[first_load + kb // ROWS_PER_LOAD]
                        for j in range(per_bank):
                            c = b * per_bank + j
                            nc.tensor.matmul(
                                banks[b][:, j * B : (j + 1) * B],
                                w_rows[:, kb % ROWS_PER_LOAD, c * P : (c + 1) * P],
                                h_in[:, kb, :],
                                start=(kb == 0 and j == 0),
                                stop=(kb == n_in - 1 and j == per_bank - 1),
                            )
                if (first_kb + together) % ROWS_PER_LOAD == 0:
                    load_next()
            for b in range(n_banks):
                blocks = slice(b * per_bank, (b + 1) * per_bank)
                acc = banks[b][:].rearrange("p (c n) -> p c n", c=per_bank)
                c0 = first_row[bias_name] + b * per_bank
                bias = bias_cols[:, c0 : c0 + per_bank].unsqueeze(2).to_broadcast([P, per_bank, B])
                if h_out is None:
                    staged = staging.tile([P, per_bank, B], F32, name="staged")
                    if b % 2 == 0:
                        for j in range(per_bank):
                            nc.scalar.activation(
                                staged[:, j, :],
                                banks[b][:, j * B : (j + 1) * B],
                                IDENTITY,
                                bias=bias_cols[:, c0 + j : c0 + j + 1],
                            )
                    else:
                        nc.vector.tensor_tensor(staged[:], acc, bias, ADD)
                    nc.sync.dma_start(out.rearrange("(c p) n -> p c n", p=P)[:, blocks, :], staged[:])
                else:
                    nc.vector.tensor_tensor(h_out[:, blocks, :], acc, bias, ADD)
            return first_load + n_in // ROWS_PER_LOAD

        h2 = held.tile([P, H // P, B], BF16, name="h2")
        h3 = held.tile([P, H // P, B], BF16, name="h3")
        h4 = held.tile([P, H // P, B], BF16, name="h4")
        load = linear(h1, 0, "b2", h2, 1, PER_BANK)
        load = linear(h2, load, "b3", h3, ROWS_PER_LOAD, PER_BANK)
        load = linear(h3, load, "b4", h4, ROWS_PER_LOAD, PER_BANK)
        linear(h4, load, "b5", None, ROWS_PER_LOAD, PER_BANK_LAST)
